import numpy as np
import ml_dtypes


def mxq(x, axis, fmt="e4m3"):
    dtype, down = {"e4m3": (ml_dtypes.float8_e4m3fn, 7), "e5m2": (ml_dtypes.float8_e5m2, 14)}[fmt]
    v = np.moveaxis(np.asarray(x, np.float32).astype(ml_dtypes.bfloat16).astype(np.float64), axis, -1)
    blocks = v.reshape(v.shape[:-1] + (-1, 32))
    amax = np.abs(blocks).max(-1, keepdims=True)
    byte = np.maximum(np.where(amax > 0, np.frexp(amax)[1] - 1 + 127, 0) - down, 1)
    scale = np.exp2(byte - 127.0)
    codes = (blocks / scale).astype(np.float32).astype(dtype).astype(np.float64)
    return np.moveaxis((codes * scale).reshape(v.shape), -1, axis)


WIDE = False


def mx_kscale(k):
    if not WIDE:
        return np.ones(k)
    levels = np.array([10, -10, 5, -5, 0])
    if k % 512:
        return np.exp2(np.random.permutation(np.resize(levels, k // 32))).repeat(32)
    a = np.empty((k // 512, 16))
    for p in range(k // 512):
        a[p, :8] = np.random.permutation(np.resize(levels, 8))
        for g in range(8):
            far = levels[np.abs(levels - a[p, g]) >= 10]
            a[p, g + 8] = far[np.random.randint(len(far))]
    return np.exp2(a.ravel()).repeat(32)


BF16 = ml_dtypes.bfloat16


def bf(x):
    return np.asarray(x, np.float32).astype(BF16)


def f64(x):
    return np.asarray(x).astype(np.float64)


NQ, NK, QS, KS, F, DEG = 4096, 1024, 1024, 512, 512, 32
EPS = 1e-5
SLOPE = 0.01


def leaky(v):
    return np.where(v >= 0, v, SLOPE * v)


def setup_inputs():
    s, t = mx_kscale(QS), mx_kscale(F)
    return {"x": bf(np.random.standard_normal((NQ, QS)) * s),
            "w1": bf(np.random.standard_normal((QS, F)) / np.sqrt(QS) / s[:, None] * t),
            "b1": bf(np.random.standard_normal(F) * 0.5 * t),
            "w2": bf(np.random.standard_normal((F, F)) / np.sqrt(F) / t[:, None]),
            "b2": bf(np.random.standard_normal(F) * 0.5),
            "gamma": bf(1.0 + 0.1 * np.random.standard_normal(F)),
            "beta": bf(0.1 * np.random.standard_normal(F))}


def reference(x, w1, b1, w2, b2, gamma, beta):
    h = leaky((mxq(f64(x), 1, "e4m3") @ mxq(f64(w1), 0, "e4m3")) + f64(b1))
    h = leaky((mxq(h, 1, "e4m3") @ mxq(f64(w2), 0, "e4m3")) + f64(b2))
    mean = h.mean(axis=0)
    var = h.var(axis=0)
    return f64(gamma) * (h - mean) / np.sqrt(var + EPS) + f64(beta)

@@ -1,0 +1,383 @@
+from contextlib import ExitStack
+
+import concourse.masks as masks
+import concourse.mybir as mybir
+
+F32 = mybir.dt.float32
+BF16 = mybir.dt.bfloat16
+U32 = mybir.dt.uint32
+U8 = mybir.dt.uint8
+FP8X4 = mybir.dt.float8_e4m3fn_x4
+ALU = mybir.AluOpType
+ACT = mybir.ActivationFunctionType
+
+P = 128
+NQ, QS, F = 4096, 1024, 512
+CH = 512
+NCH = NQ // CH
+RT = CH // P
+NI = NQ // P
+FT = F // P
+EPS = 1e-5
+SLOPE = 0.01
+FLOPS = 2 * NQ * QS * F + 2 * NQ * F * F
+
+MANUAL = False
+GB = 2
+PLAG = 2
+EXTRA = {6: 1, 7: 1}
+
+
+def tile_attention_prop_pa_t_kernel(tc, x, w1, b1, w2, b2, gamma, beta, out):
+    nc = tc.nc
+    with ExitStack() as ctx:
+        const = ctx.enter_context(tc.tile_pool(name="const", bufs=1))
+        wts = ctx.enter_context(tc.tile_pool(name="wts", bufs=1))
+        xin = ctx.enter_context(tc.tile_pool(name="xin", bufs=4))
+        xgp = ctx.enter_context(tc.tile_pool(name="xgp", bufs=2))
+        xqp = ctx.enter_context(tc.tile_pool(name="xqp", bufs=3))
+        v1p = ctx.enter_context(tc.tile_pool(name="v1p", bufs=2))
+        h1gp = ctx.enter_context(tc.tile_pool(name="h1gp", bufs=2))
+        h1qp = ctx.enter_context(tc.tile_pool(name="h1qp", bufs=1))
+        h2p = ctx.enter_context(tc.tile_pool(name="h2p", bufs=1))
+        s2p = ctx.enter_context(tc.tile_pool(name="s2p", bufs=6))
+        ostp = ctx.enter_context(tc.tile_pool(name="ostp", bufs=6))
+        pt = ctx.enter_context(tc.psum_pool(name="pt", bufs=4))
+        pm = ctx.enter_context(tc.psum_pool(name="pm", bufs=4))
+        if MANUAL:
+            ctx.enter_context(tc.manual_schedule())
+
+        x_v = x.rearrange("(p i) k -> p i k", i=NI)
+        out_v = out.rearrange("(p i) f -> p i f", i=NI)
+
+        b1t = const.tile([P, FT], BF16, name="b1t")
+        b2t = const.tile([P, FT], BF16, name="b2t")
+        gat = const.tile([P, FT], BF16, name="gat")
+        bet = const.tile([P, FT], BF16, name="bet")
+
+        w1raw = wts.tile([P, 4096], BF16, name="w1raw")
+        w1_v = w1.rearrange("(g q j) c -> q g j c", g=2, q=P, j=4)
+
+        def load_w1(g):
+            nc.sync.dma_start(
+                out=w1raw[:, 2048 * g : 2048 * (g + 1)].rearrange("p (j c) -> p j c", j=4),
+                in_=w1_v[:, g],
+            )
+
+        xt_tiles = {}
+
+        def load_x(c):
+            xc = xin.tile([P, RT * QS], BF16, name="xc")
+            xt_tiles[c] = xc
+            if c == 0:
+                for i in range(RT):
+                    nc.sync.dma_start(out=xc[:, QS * i : QS * (i + 1)], in_=x_v[:, i, :])
+                    if i % 2 == 1:
+                        load_w1(i // 2)
+            else:
+                nc.sync.dma_start(
+                    out=xc[:].rearrange("p (i k) -> p i k", i=RT), in_=x_v[:, RT * c : RT * (c + 1), :]
+                )
+
+        load_x(0)
+        load_x(1)
+        w2raw = wts.tile([P, 2048], BF16, name="w2raw")
+        nc.sync.dma_start(
+            out=w2raw[:].rearrange("p (t c) -> p t c", t=4), in_=w2.rearrange("(p t) c -> p t c", t=4)
+        )
+        nc.sync.dma_start(out=b1t[:], in_=b1.rearrange("(p t) -> p t", t=FT))
+        load_x(2)
+        with nc.allow_non_contiguous_dma(reason="512 values, one to a partition and feature tile"):
+            nc.sync.dma_start(out=b2t[:], in_=b2.rearrange("(t p) -> p t", p=P))
+            nc.sync.dma_start(out=gat[:], in_=gamma.rearrange("(t p) -> p t", p=P))
+            nc.sync.dma_start(out=bet[:], in_=beta.rearrange("(t p) -> p t", p=P))
+        load_x(3)
+
+        ident = const.tile([P, P], F32, name="ident")
+        masks.make_identity(nc, ident[:])
+        mhalf = const.tile([P, 1], F32, name="mhalf")
+        nc.gpsimd.memset(mhalf[:], -0.5)
+        b1f = const.tile([P, FT], F32, name="b1f")
+        b2f = const.tile([P, FT], F32, name="b2f")
+        b2s = const.tile([P, FT], F32, name="b2s")
+        gaf = const.tile([P, FT], F32, name="gaf")
+        bef = const.tile([P, FT], F32, name="bef")
+        nc.gpsimd.tensor_copy(out=b1f[:], in_=b1t[:])
+        nc.gpsimd.tensor_copy(out=b2f[:], in_=b2t[:])
+        nc.gpsimd.tensor_scalar(out=b2s[:], in0=b2t[:], scalar1=SLOPE, scalar2=0.0, op0=ALU.mult, op1=ALU.add)
+        nc.gpsimd.tensor_copy(out=gaf[:], in_=gat[:])
+        nc.gpsimd.tensor_copy(out=bef[:], in_=bet[:])
+
+        w1g = wts.tile([P, 4096], BF16, name="w1g", align_bytes=64)
+        w1q = wts.tile([P, 1024], U32, name="w1q", align_bytes=64)
+        w1s = wts.tile([P, 1024], U8, name="w1s", align_bytes=64)
+
+        def prep_w1():
+            for g in range(2):
+                nc.vector.tensor_copy(
+                    out=w1g[:, 2048 * g : 2048 * (g + 1)].rearrange("p (t m j) -> p t m j", t=4, m=P, j=4),
+                    in_=w1raw[:, 2048 * g : 2048 * (g + 1)].rearrange("p (j m t) -> p t m j", j=4, m=P, t=4),
+                )
+            for g in range(2):
+                nc.vector.quantize_mx(
+                    out=w1q[:, 512 * g : 512 * (g + 1)].bitcast(FP8X4),
+                    scales=w1s[:, 512 * g : 512 * (g + 1)],
+                    in_=w1g[:, 2048 * g : 2048 * (g + 1)],
+                )
+
+        w2g = wts.tile([P, 2048], BF16, name="w2g", align_bytes=64)
+        w2q = wts.tile([P, 512], U32, name="w2q", align_bytes=64)
+        w2s = wts.tile([P, 512], U8, name="w2s", align_bytes=64)
+
+        def prep_w2():
+            nc.vector.tensor_copy(
+                out=w2g[:].rearrange("p (c t) -> p c t", t=4), in_=w2raw[:].rearrange("p (t c) -> p c t", t=4)
+            )
+            nc.vector.quantize_mx(out=w2q[:].bitcast(FP8X4), scales=w2s[:], in_=w2g[:])
+
+        xbanks = {}
+        xgs = {}
+        xqs = {}
+        m1banks = {}
+        v1s = {}
+        h1gs = {}
+        h1qs = {}
+        m2banks = {}
+        s2s = {}
+        h2s = {}
+        obanks = {}
+        stats = [const.tile([P, 6 * NCH], F32, name="stats%d" % t) for t in range(FT)]
+        coefs = {}
+
+        def t_x(c):
+            xw = xt_tiles[c][:].bitcast(F32)
+            for i in range(RT):
+                bank = pt.tile([P, 512], F32, name="ptb")
+                xbanks[(c, i)] = bank
+                for q in range(4):
+                    nc.tensor.transpose(
+                        bank[:, P * q : P * (q + 1)],
+                        xw[:, 512 * i + 256 * (q // 2) + q % 2 : 512 * i + 256 * (q // 2 + 1) : 2],
+                        ident[:],
+                    )
+            if c + 4 < NCH:
+                load_x(c + 4)
+
+        def xe(c):
+            xg = xgp.tile([P, 4096], BF16, name="xg", align_bytes=64)
+            xgs[c] = xg
+            xg32 = xg[:].bitcast(F32).rearrange("p (g r u) -> p g r u", g=2, r=CH, u=2)
+            for i in range(RT):
+                nc.scalar.copy(
+                    out=xg32[:, :, P * i : P * (i + 1), :],
+                    in_=xbanks[(c, i)][:].rearrange("p (g u r) -> p g r u", g=2, u=2, r=P),
+                )
+
+        def qx(c):
+            xq = xqp.tile([P, 1024], U32, name="xq", align_bytes=64)
+            xs = xqp.tile([P, 1024], U8, name="xs", align_bytes=64)
+            xqs[c] = (xq, xs)
+            nc.vector.quantize_mx(out=xq[:].bitcast(FP8X4), scales=xs[:], in_=xgs[c][:])
+
+        def m1(c):
+            xq, xs = xqs[c]
+            for t in range(FT):
+                bank = pm.tile([P, 512], F32, name="pmb")
+                m1banks[(c, t)] = bank
+                for g in range(2):
+                    lo = 512 * g + P * t
+                    nc.tensor.matmul_mx(
+                        out=bank[:],
+                        lhsT=w1q[:, lo : lo + P].bitcast(FP8X4),
+                        lhsT_scale=w1s[:, lo : lo + P],
+                        rhs=xq[:, 512 * g : 512 * (g + 1)].bitcast(FP8X4),
+                        rhs_scale=xs[:, 512 * g : 512 * (g + 1)],
+                        start=(g == 0),
+                        stop=(g == 1),
+                    )
+
+        def bias1(c):
+            v1 = v1p.tile([P, 2048], F32, name="v1")
+            v1s[c] = v1
+            for t in range(FT):
+                nc.scalar.activation(
+                    out=v1[:, 512 * t : 512 * (t + 1)],
+                    in_=m1banks[(c, t)][:],
+                    func=ACT.Identity,
+                    bias=b1f[:, t : t + 1],
+                    scale=1.0,
+                )
+
+        def st1(c):
+            h1g = h1gp.tile([P, 2048], BF16, name="h1g", align_bytes=64)
+            h1gs[c] = h1g
+            v = v1s[c][:].rearrange("p (t w) -> p w t", t=FT)
+            nc.vector.scalar_tensor_tensor(
+                out=h1g[:].rearrange("p (w t) -> p w t", t=FT), in0=v, scalar=SLOPE, in1=v, op0=ALU.mult, op1=ALU.max
+            )
+
+        def qh(c):
+            hq = h1qp.tile([P, 512], U32, name="h1q%d" % c, align_bytes=64)
+            hs = h1qp.tile([P, 512], U8, name="h1s%d" % c, align_bytes=64)
+            h1qs[c] = (hq, hs)
+            nc.vector.quantize_mx(out=hq[:].bitcast(FP8X4), scales=hs[:], in_=h1gs[c][:])
+
+        def m2(c, t):
+            hq, hs = h1qs[c]
+            bank = pm.tile([P, 512], F32, name="pmb")
+            m2banks[(c, t)] = bank
+            nc.tensor.matmul_mx(
+                out=bank[:],
+                lhsT=w2q[:, P * t : P * (t + 1)].bitcast(FP8X4),
+                lhsT_scale=w2s[:, P * t : P * (t + 1)],
+                rhs=hq[:].bitcast(FP8X4),
+                rhs_scale=hs[:],
+                start=True,
+                stop=True,
+            )
+
+        def s2(c, t, whole):
+            s = s2p.tile([P, 512], F32, name="s2")
+            s2s[(c, t)] = s
+            if whole:
+                nc.scalar.activation(
+                    out=s[:], in_=m2banks[(c, t)][:], func=ACT.Identity, bias=b2f[:, t : t + 1], scale=1.0
+                )
+            else:
+                nc.scalar.activation(
+                    out=s[:], in_=m2banks[(c, t)][:], func=ACT.Identity, bias=b2s[:, t : t + 1], scale=SLOPE
+                )
+
+        def st2(c, t, whole):
+            h2 = h2p.tile([P, 512], F32, name="h2_%d_%d" % (t, c))
+            h2s[(c, t)] = h2
+            if whole:
+                nc.vector.scalar_tensor_tensor(
+                    out=h2[:], in0=s2s[(c, t)][:], scalar=SLOPE, in1=s2s[(c, t)][:], op0=ALU.mult, op1=ALU.max
+                )
+            else:
+                nc.vector.scalar_tensor_tensor(
+                    out=h2[:],
+                    in0=m2banks[(c, t)][:],
+                    scalar=b2f[:, t : t + 1],
+                    in1=s2s[(c, t)][:],
+                    op0=ALU.add,
+                    op1=ALU.max,
+                )
+            nc.vector.bn_stats(out=stats[t][:, 6 * c : 6 * (c + 1)], in_=h2[:])
+
+        def agg(t):
+            mv = const.tile([P, 2], F32, name="mv%d" % t)
+            ve = const.tile([P, 1], F32, name="ve%d" % t)
+            rstd = const.tile([P, 1], F32, name="rstd%d" % t)
+            ca = const.tile([P, 1], F32, name="ca%d" % t)
+            ma = const.tile([P, 1], F32, name="ma%d" % t)
+            cb = const.tile([P, 1], F32, name="cb%d" % t)
+            coefs[t] = (ca, cb)
+            nc.vector.bn_aggr(out=mv[:], in_=stats[t][:])
+            nc.gpsimd.tensor_scalar(out=ve[:], in0=mv[:, 1:2], scalar1=1.0, scalar2=EPS, op0=ALU.mult, op1=ALU.add)
+            nc.gpsimd.tensor_tensor(out=rstd[:], in0=ve[:], in1=mhalf[:], op=ALU.pow)
+            nc.gpsimd.tensor_tensor(out=ca[:], in0=rstd[:], in1=gaf[:, t : t + 1], op=ALU.mult)
+            nc.gpsimd.tensor_tensor(out=ma[:], in0=mv[:, 0:1], in1=ca[:], op=ALU.mult)
+            nc.gpsimd.tensor_tensor(out=cb[:], in0=bef[:, t : t + 1], in1=ma[:], op=ALU.subtract)
+
+        def norm(c, t, eng):
+            ca, cb = coefs[t]
+            h2 = h2s[(c, t)]
+            eng.tensor_scalar(out=h2[:], in0=h2[:], scalar1=ca[:, 0:1], scalar2=cb[:, 0:1], op0=ALU.mult, op1=ALU.add)
+
+        def t_o(c, t):
+            bank = pt.tile([P, 512], F32, name="ptb")
+            obanks[(c, t)] = bank
+            h2 = h2s[(c, t)]
+            for i in range(RT):
+                nc.tensor.transpose(bank[:, P * i : P * (i + 1)], h2[:, P * i : P * (i + 1)], ident[:])
+
+        def ex(c, t):
+            ost = ostp.tile([P, 512], F32, name="ost")
+            if t == FT - 1 and c % 2 == 1:
+                nc.vector.tensor_copy(out=ost[:], in_=obanks[(c, t)][:])
+            else:
+                nc.scalar.copy(out=ost[:], in_=obanks[(c, t)][:])
+            nc.sync.dma_start(
+                out=out_v[:, RT * c : RT * (c + 1), P * t : P * (t + 1)], in_=ost[:].rearrange("p (i f) -> p i f", i=RT)
+            )
+
+        units = [(c, t) for t in range(FT) for c in range(NCH)]
+        pos = {"m": 0, "s": 0, "v": 0, "p": 0, "e": 0, "step": 0}
+        agg_step = {}
+
+        whole_of = {}
+
+        def v_units():
+            while pos["v"] < pos["s"]:
+                c, t = units[pos["v"]]
+                st2(c, t, whole_of[(c, t)])
+                pos["v"] += 1
+                if c == NCH - 1:
+                    agg(t)
+                    agg_step[t] = pos["step"]
+                    for cc in range(NCH):
+                        norm(cc, t, nc.gpsimd if t < FT - 1 else nc.vector)
+
+        t_x(0)
+        xe(0)
+        prep_w1()
+        t_x(1)
+        qx(0)
+        xe(1)
+        m1(0)
+        t_x(2)
+        bias1(0)
+        qx(1)
+        prep_w2()
+        xe(2)
+        for n in range(NCH):
+            pos["step"] += 1
+            if n + 1 < NCH:
+                m1(n + 1)
+            if n + 3 < NCH:
+                t_x(n + 3)
+            mu = []
+            for j in range((1 if n >= 1 else 0) + EXTRA.get(n, 0)):
+                if units[pos["m"]][0] <= n - 1:
+                    mu.append(units[pos["m"]])
+                    pos["m"] += 1
+            for c, t in mu:
+                m2(c, t)
+            st1(n)
+            v_units()
+            qh(n)
+            if n + 2 < NCH:
+                qx(n + 2)
+            if n + 1 < NCH:
+                bias1(n + 1)
+            if n + 3 < NCH:
+                xe(n + 3)
+            for c, t in mu:
+                s2(c, t, True)
+                whole_of[(c, t)] = True
+                pos["s"] += 1
+        while pos["v"] < len(units) or pos["e"] < len(units):
+            pos["step"] += 1
+            mu = units[pos["m"] : pos["m"] + GB]
+            pos["m"] += len(mu)
+            for c, t in mu:
+                m2(c, t)
+            pa = []
+            for j in range(GB):
+                if pos["p"] < len(units):
+                    u = units[pos["p"]]
+                    if u[1] in agg_step and pos["step"] - agg_step[u[1]] >= PLAG:
+                        pa.append(u)
+                        pos["p"] += 1
+            for c, t in pa:
+                t_o(c, t)
+            v_units()
+            for c, t in mu:
+                s2(c, t, False)
+                whole_of[(c, t)] = False
+                pos["s"] += 1
+            for c, t in pa:
+                ex(c, t)
+                pos["e"] += 1

@@ -22,10 +22,7 @@ EPS = 1e-5
 SLOPE = 0.01
 FLOPS = 2 * NQ * QS * F + 2 * NQ * F * F
 
-MANUAL = False
 GB = 2
-PLAG = 2
-EXTRA = {6: 1, 7: 1}
 
 
 def tile_attention_prop_pa_t_kernel(tc, x, w1, b1, w2, b2, gamma, beta, out):
@@ -44,8 +41,7 @@ def tile_attention_prop_pa_t_kernel(tc, x, w1, b1, w2, b2, gamma, beta, out):
         ostp = ctx.enter_context(tc.tile_pool(name="ostp", bufs=6))
         pt = ctx.enter_context(tc.psum_pool(name="pt", bufs=4))
         pm = ctx.enter_context(tc.psum_pool(name="pm", bufs=4))
-        if MANUAL:
-            ctx.enter_context(tc.manual_schedule())
+        ctx.enter_context(tc.manual_schedule())
 
         x_v = x.rearrange("(p i) k -> p i k", i=NI)
         out_v = out.rearrange("(p i) f -> p i f", i=NI)
@@ -71,9 +67,9 @@ def tile_attention_prop_pa_t_kernel(tc, x, w1, b1, w2, b2, gamma, beta, out):
             xt_tiles[c] = xc
             if c == 0:
                 for i in range(RT):
-                    nc.sync.dma_start(out=xc[:, QS * i : QS * (i + 1)], in_=x_v[:, i, :])
-                    if i % 2 == 1:
+                    if i % 2 == 0:
                         load_w1(i // 2)
+                    nc.sync.dma_start(out=xc[:, QS * i : QS * (i + 1)], in_=x_v[:, i, :])
             else:
                 nc.sync.dma_start(
                     out=xc[:].rearrange("p (i k) -> p i k", i=RT), in_=x_v[:, RT * c : RT * (c + 1), :]
@@ -112,27 +108,29 @@ def tile_attention_prop_pa_t_kernel(tc, x, w1, b1, w2, b2, gamma, beta, out):
         w1q = wts.tile([P, 1024], U32, name="w1q", align_bytes=64)
         w1s = wts.tile([P, 1024], U8, name="w1s", align_bytes=64)
 
-        def prep_w1():
-            for g in range(2):
-                nc.vector.tensor_copy(
-                    out=w1g[:, 2048 * g : 2048 * (g + 1)].rearrange("p (t m j) -> p t m j", t=4, m=P, j=4),
-                    in_=w1raw[:, 2048 * g : 2048 * (g + 1)].rearrange("p (j m t) -> p t m j", j=4, m=P, t=4),
-                )
-            for g in range(2):
-                nc.vector.quantize_mx(
-                    out=w1q[:, 512 * g : 512 * (g + 1)].bitcast(FP8X4),
-                    scales=w1s[:, 512 * g : 512 * (g + 1)],
-                    in_=w1g[:, 2048 * g : 2048 * (g + 1)],
-                )
+        def copy_w1(g):
+            nc.vector.tensor_copy(
+                out=w1g[:, 2048 * g : 2048 * (g + 1)].rearrange("p (t m j) -> p t m j", t=4, m=P, j=4),
+                in_=w1raw[:, 2048 * g : 2048 * (g + 1)].rearrange("p (j m t) -> p t m j", j=4, m=P, t=4),
+            )
+
+        def quant_w1(g):
+            nc.vector.quantize_mx(
+                out=w1q[:, 512 * g : 512 * (g + 1)].bitcast(FP8X4),
+                scales=w1s[:, 512 * g : 512 * (g + 1)],
+                in_=w1g[:, 2048 * g : 2048 * (g + 1)],
+            )
 
         w2g = wts.tile([P, 2048], BF16, name="w2g", align_bytes=64)
         w2q = wts.tile([P, 512], U32, name="w2q", align_bytes=64)
         w2s = wts.tile([P, 512], U8, name="w2s", align_bytes=64)
 
-        def prep_w2():
+        def copy_w2():
             nc.vector.tensor_copy(
                 out=w2g[:].rearrange("p (c t) -> p c t", t=4), in_=w2raw[:].rearrange("p (t c) -> p c t", t=4)
             )
+
+        def quant_w2():
             nc.vector.quantize_mx(out=w2q[:].bitcast(FP8X4), scales=w2s[:], in_=w2g[:])
 
         xbanks = {}
@@ -150,6 +148,8 @@ def tile_attention_prop_pa_t_kernel(tc, x, w1, b1, w2, b2, gamma, beta, out):
         coefs = {}
 
         def t_x(c):
+            if c >= NCH:
+                return
             xw = xt_tiles[c][:].bitcast(F32)
             for i in range(RT):
                 bank = pt.tile([P, 512], F32, name="ptb")
@@ -163,11 +163,14 @@ def tile_attention_prop_pa_t_kernel(tc, x, w1, b1, w2, b2, gamma, beta, out):
             if c + 4 < NCH:
                 load_x(c + 4)
 
-        def xe(c):
-            xg = xgp.tile([P, 4096], BF16, name="xg", align_bytes=64)
-            xgs[c] = xg
-            xg32 = xg[:].bitcast(F32).rearrange("p (g r u) -> p g r u", g=2, r=CH, u=2)
-            for i in range(RT):
+        def xe(c, tiles):
+            if c >= NCH:
+                return
+            if 0 in tiles:
+                xg = xgp.tile([P, 4096], BF16, name="xg", align_bytes=64)
+                xgs[c] = xg
+            xg32 = xgs[c][:].bitcast(F32).rearrange("p (g r u) -> p g r u", g=2, r=CH, u=2)
+            for i in tiles:
                 nc.scalar.copy(
                     out=xg32[:, :, P * i : P * (i + 1), :],
                     in_=xbanks[(c, i)][:].rearrange("p (g u r) -> p g r u", g=2, u=2, r=P),
@@ -264,27 +267,29 @@ def tile_attention_prop_pa_t_kernel(tc, x, w1, b1, w2, b2, gamma, beta, out):
                     op0=ALU.add,
                     op1=ALU.max,
                 )
-            nc.vector.bn_stats(out=stats[t][:, 6 * c : 6 * (c + 1)], in_=h2[:])
+
+        def bn(c, t):
+            nc.vector.bn_stats(out=stats[t][:, 6 * c : 6 * (c + 1)], in_=h2s[(c, t)][:])
 
         def agg(t):
             mv = const.tile([P, 2], F32, name="mv%d" % t)
             ve = const.tile([P, 1], F32, name="ve%d" % t)
             rstd = const.tile([P, 1], F32, name="rstd%d" % t)
             ca = const.tile([P, 1], F32, name="ca%d" % t)
-            ma = const.tile([P, 1], F32, name="ma%d" % t)
             cb = const.tile([P, 1], F32, name="cb%d" % t)
             coefs[t] = (ca, cb)
             nc.vector.bn_aggr(out=mv[:], in_=stats[t][:])
             nc.gpsimd.tensor_scalar(out=ve[:], in0=mv[:, 1:2], scalar1=1.0, scalar2=EPS, op0=ALU.mult, op1=ALU.add)
             nc.gpsimd.tensor_tensor(out=rstd[:], in0=ve[:], in1=mhalf[:], op=ALU.pow)
             nc.gpsimd.tensor_tensor(out=ca[:], in0=rstd[:], in1=gaf[:, t : t + 1], op=ALU.mult)
-            nc.gpsimd.tensor_tensor(out=ma[:], in0=mv[:, 0:1], in1=ca[:], op=ALU.mult)
-            nc.gpsimd.tensor_tensor(out=cb[:], in0=bef[:, t : t + 1], in1=ma[:], op=ALU.subtract)
+            nc.gpsimd.tensor_scalar(
+                out=cb[:], in0=mv[:, 0:1], scalar1=ca[:, 0:1], scalar2=bef[:, t : t + 1], op0=ALU.mult, op1=ALU.subtract
+            )
 
         def norm(c, t, eng):
             ca, cb = coefs[t]
             h2 = h2s[(c, t)]
-            eng.tensor_scalar(out=h2[:], in0=h2[:], scalar1=ca[:, 0:1], scalar2=cb[:, 0:1], op0=ALU.mult, op1=ALU.add)
+            eng.tensor_scalar(out=h2[:], in0=h2[:], scalar1=ca[:, 0:1], scalar2=cb[:, 0:1], op0=ALU.mult, op1=ALU.subtract)
 
         def t_o(c, t):
             bank = pt.tile([P, 512], F32, name="ptb")
@@ -303,81 +308,99 @@ def tile_attention_prop_pa_t_kernel(tc, x, w1, b1, w2, b2, gamma, beta, out):
                 out=out_v[:, RT * c : RT * (c + 1), P * t : P * (t + 1)], in_=ost[:].rearrange("p (i f) -> p i f", i=RT)
             )
 
-        units = [(c, t) for t in range(FT) for c in range(NCH)]
-        pos = {"m": 0, "s": 0, "v": 0, "p": 0, "e": 0, "step": 0}
-        agg_step = {}
-
+        waiting = [(c, t) for t in range(FT) for c in range(NCH)]
+        quantised = []
+        statq = []
+        done_stats = []
+        outq = []
         whole_of = {}
+        pos = {"g": 0}
 
-        def v_units():
-            while pos["v"] < pos["s"]:
-                c, t = units[pos["v"]]
-                st2(c, t, whole_of[(c, t)])
-                pos["v"] += 1
-                if c == NCH - 1:
+        def take(n):
+            got = []
+            for u in list(waiting):
+                if len(got) < n and u[0] in quantised:
+                    got.append(u)
+                    waiting.remove(u)
+            return got
+
+        def flush_bn(keep):
+            while len(statq) > keep:
+                c, t = statq.pop(0)
+                bn(c, t)
+                done_stats.append((c, t))
+                if len([u for u in done_stats if u[1] == t]) == NCH:
                     agg(t)
-                    agg_step[t] = pos["step"]
                     for cc in range(NCH):
                         norm(cc, t, nc.gpsimd if t < FT - 1 else nc.vector)
+                        outq.append(((cc, t), pos["g"]))
 
+        def do_st2(u):
+            st2(u[0], u[1], whole_of[u])
+            statq.append(u)
+
+        RIDE = {2: 1, 3: 1, 4: 1, 5: 1, 6: 1, 7: 1}
         t_x(0)
-        xe(0)
-        prep_w1()
+        copy_w1(0)
+        quant_w1(0)
+        copy_w1(1)
+        xe(0, range(RT))
+        quant_w1(1)
         t_x(1)
         qx(0)
-        xe(1)
         m1(0)
-        t_x(2)
-        bias1(0)
-        qx(1)
-        prep_w2()
-        xe(2)
+        xe(1, range(RT))
+        copy_w2()
+        prev = []
         for n in range(NCH):
-            pos["step"] += 1
+            t_x(n + 2)
+            units = take(RIDE.get(n, 0))
+            for u in prev:
+                do_st2(u)
+            if n + 1 < NCH:
+                qx(n + 1)
+            if n == 0:
+                quant_w2()
+            if n >= 1:
+                qh(n - 1)
+            flush_bn(0)
+            bias1(n)
+            st1(n)
+            xe(n + 2, [0])
+            for u in units:
+                m2(u[0], u[1])
+                whole_of[u] = True
+                s2(u[0], u[1], True)
             if n + 1 < NCH:
                 m1(n + 1)
-            if n + 3 < NCH:
-                t_x(n + 3)
-            mu = []
-            for j in range((1 if n >= 1 else 0) + EXTRA.get(n, 0)):
-                if units[pos["m"]][0] <= n - 1:
-                    mu.append(units[pos["m"]])
-                    pos["m"] += 1
-            for c, t in mu:
-                m2(c, t)
-            st1(n)
-            v_units()
-            qh(n)
-            if n + 2 < NCH:
-                qx(n + 2)
-            if n + 1 < NCH:
-                bias1(n + 1)
-            if n + 3 < NCH:
-                xe(n + 3)
-            for c, t in mu:
-                s2(c, t, True)
-                whole_of[(c, t)] = True
-                pos["s"] += 1
-        while pos["v"] < len(units) or pos["e"] < len(units):
-            pos["step"] += 1
-            mu = units[pos["m"] : pos["m"] + GB]
-            pos["m"] += len(mu)
-            for c, t in mu:
-                m2(c, t)
-            pa = []
-            for j in range(GB):
-                if pos["p"] < len(units):
-                    u = units[pos["p"]]
-                    if u[1] in agg_step and pos["step"] - agg_step[u[1]] >= PLAG:
-                        pa.append(u)
-                        pos["p"] += 1
-            for c, t in pa:
-                t_o(c, t)
-            v_units()
-            for c, t in mu:
-                s2(c, t, False)
-                whole_of[(c, t)] = False
-                pos["s"] += 1
-            for c, t in pa:
-                ex(c, t)
-                pos["e"] += 1
+            xe(n + 2, [1, 2, 3])
+            prev = units
+            if n >= 1:
+                quantised.append(n - 1)
+        for u in prev:
+            do_st2(u)
+        qh(NCH - 1)
+        quantised.append(NCH - 1)
+        prev = []
+        LAG = 2
+        while waiting or prev or statq or outq:
+            pos["g"] += 1
+            units = take(GB)
+            for u in units:
+                m2(u[0], u[1])
+                whole_of[u] = False
+            outs = []
+            while outq and len(outs) < GB and (pos["g"] - outq[0][1] >= LAG or not waiting):
+                outs.append(outq.pop(0)[0])
+            for u in prev:
+                do_st2(u)
+                flush_bn(1)
+            if not units:
+                flush_bn(0)
+            for u in outs:
+                t_o(u[0], u[1])
+            for u in units:
+                s2(u[0], u[1], False)
+            for u in outs:
+                ex(u[0], u[1])
+            prev = units

@@ -96,12 +96,21 @@ def tile_attention_prop_pa_t_kernel(tc, x, w1, b1, w2, b2, gamma, beta, out):
         b1f = const.tile([P, FT], F32, name="b1f")
         b2f = const.tile([P, FT], F32, name="b2f")
         b2s = const.tile([P, FT], F32, name="b2s")
-        gaf = const.tile([P, FT], F32, name="gaf")
+        gaf = const.tile([P, 2 * FT], F32, name="gaf")
         bef = const.tile([P, FT], F32, name="bef")
         nc.gpsimd.tensor_copy(out=b1f[:], in_=b1t[:])
         nc.gpsimd.tensor_copy(out=b2f[:], in_=b2t[:])
         nc.gpsimd.tensor_scalar(out=b2s[:], in0=b2t[:], scalar1=SLOPE, scalar2=0.0, op0=ALU.mult, op1=ALU.add)
-        nc.gpsimd.tensor_copy(out=gaf[:], in_=gat[:])
+        for t in range(FT):
+            for j in range(2):
+                nc.gpsimd.tensor_scalar(
+                    out=gaf[:, 2 * t + j : 2 * t + j + 1],
+                    in0=gat[:, t : t + 1],
+                    scalar1=1.0 - 2.0 * j,
+                    scalar2=0.0,
+                    op0=ALU.mult,
+                    op1=ALU.add,
+                )
         nc.gpsimd.tensor_copy(out=bef[:], in_=bet[:])
 
         w1g = wts.tile([P, 4096], BF16, name="w1g", align_bytes=64)
@@ -275,21 +284,23 @@ def tile_attention_prop_pa_t_kernel(tc, x, w1, b1, w2, b2, gamma, beta, out):
             mv = const.tile([P, 2], F32, name="mv%d" % t)
             ve = const.tile([P, 1], F32, name="ve%d" % t)
             rstd = const.tile([P, 1], F32, name="rstd%d" % t)
-            ca = const.tile([P, 1], F32, name="ca%d" % t)
+            ca = const.tile([P, 2], F32, name="ca%d" % t)
             cb = const.tile([P, 1], F32, name="cb%d" % t)
             coefs[t] = (ca, cb)
             nc.vector.bn_aggr(out=mv[:], in_=stats[t][:])
             nc.gpsimd.tensor_scalar(out=ve[:], in0=mv[:, 1:2], scalar1=1.0, scalar2=EPS, op0=ALU.mult, op1=ALU.add)
             nc.gpsimd.tensor_tensor(out=rstd[:], in0=ve[:], in1=mhalf[:], op=ALU.pow)
-            nc.gpsimd.tensor_tensor(out=ca[:], in0=rstd[:], in1=gaf[:, t : t + 1], op=ALU.mult)
             nc.gpsimd.tensor_scalar(
-                out=cb[:], in0=mv[:, 0:1], scalar1=ca[:, 0:1], scalar2=bef[:, t : t + 1], op0=ALU.mult, op1=ALU.subtract
+                out=ca[:], in0=gaf[:, 2 * t : 2 * t + 2], scalar1=rstd[:, 0:1], scalar2=0.0, op0=ALU.mult, op1=ALU.add
+            )
+            nc.gpsimd.tensor_scalar(
+                out=cb[:], in0=mv[:, 0:1], scalar1=ca[:, 1:2], scalar2=bef[:, t : t + 1], op0=ALU.mult, op1=ALU.add
             )
 
         def norm(c, t, eng):
             ca, cb = coefs[t]
             h2 = h2s[(c, t)]
-            eng.tensor_scalar(out=h2[:], in0=h2[:], scalar1=ca[:, 0:1], scalar2=cb[:, 0:1], op0=ALU.mult, op1=ALU.subtract)
+            eng.tensor_scalar(out=h2[:], in0=h2[:], scalar1=ca[:, 0:1], scalar2=cb[:, 0:1], op0=ALU.mult, op1=ALU.add)
 
         def t_o(c, t):
             bank = pt.tile([P, 512], F32, name="ptb")

@@ -100,7 +100,7 @@ def tile_attention_prop_pa_t_kernel(tc, x, w1, b1, w2, b2, gamma, beta, out):
         bef = const.tile([P, FT], F32, name="bef")
         nc.gpsimd.tensor_copy(out=b1f[:], in_=b1t[:])
         nc.gpsimd.tensor_copy(out=b2f[:], in_=b2t[:])
-        nc.gpsimd.tensor_scalar(out=b2s[:], in0=b2t[:], scalar1=SLOPE, scalar2=0.0, op0=ALU.mult, op1=ALU.add)
+        nc.gpsimd.tensor_scalar(out=b2s[:], in0=b2t[:], scalar1=SLOPE - 1.0, scalar2=0.0, op0=ALU.mult, op1=ALU.add)
         for t in range(FT):
             for j in range(2):
                 nc.gpsimd.tensor_scalar(
@@ -268,14 +268,7 @@ def tile_attention_prop_pa_t_kernel(tc, x, w1, b1, w2, b2, gamma, beta, out):
                     out=h2[:], in0=s2s[(c, t)][:], scalar=SLOPE, in1=s2s[(c, t)][:], op0=ALU.mult, op1=ALU.max
                 )
             else:
-                nc.vector.scalar_tensor_tensor(
-                    out=h2[:],
-                    in0=m2banks[(c, t)][:],
-                    scalar=b2f[:, t : t + 1],
-                    in1=s2s[(c, t)][:],
-                    op0=ALU.add,
-                    op1=ALU.max,
-                )
+                nc.vector.tensor_tensor(out=h2[:], in0=m2banks[(c, t)][:], in1=s2s[(c, t)][:], op=ALU.max)
 
         def bn(c, t):
             nc.vector.bn_stats(out=stats[t][:, 6 * c : 6 * (c + 1)], in_=h2s[(c, t)][:])
@@ -399,7 +392,7 @@ def tile_attention_prop_pa_t_kernel(tc, x, w1, b1, w2, b2, gamma, beta, out):
             units = take(GB)
             for u in units:
                 m2(u[0], u[1])
-                whole_of[u] = False
+                whole_of[u] = u[1] == 0
             outs = []
             while outq and len(outs) < GB and (pos["g"] - outq[0][1] >= LAG or not waiting):
                 outs.append(outq.pop(0)[0])
@@ -411,7 +404,7 @@ def tile_attention_prop_pa_t_kernel(tc, x, w1, b1, w2, b2, gamma, beta, out):
             for u in outs:
                 t_o(u[0], u[1])
             for u in units:
-                s2(u[0], u[1], False)
+                s2(u[0], u[1], whole_of[u])
             for u in outs:
                 ex(u[0], u[1])
             prev = units

@@ -22,6 +22,8 @@ EPS = 1e-5
 SLOPE = 0.01
 FLOPS = 2 * NQ * QS * F + 2 * NQ * F * F
 
+SQUARED = {0: (2, 4), 1: (0, 1, 2), 2: (), 3: ()}
+TAIL_C = 5
 GB = 2
 
 
@@ -38,7 +40,7 @@ def tile_attention_prop_pa_t_kernel(tc, x, w1, b1, w2, b2, gamma, beta, out):
         h1qp = ctx.enter_context(tc.tile_pool(name="h1qp", bufs=1))
         h2p = ctx.enter_context(tc.tile_pool(name="h2p", bufs=1))
         s2p = ctx.enter_context(tc.tile_pool(name="s2p", bufs=6))
-        ostp = ctx.enter_context(tc.tile_pool(name="ostp", bufs=6))
+        ostp = ctx.enter_context(tc.tile_pool(name="ostp", bufs=8))
         pt = ctx.enter_context(tc.psum_pool(name="pt", bufs=4))
         pm = ctx.enter_context(tc.psum_pool(name="pm", bufs=4))
         ctx.enter_context(tc.manual_schedule())
@@ -89,6 +91,27 @@ def tile_attention_prop_pa_t_kernel(tc, x, w1, b1, w2, b2, gamma, beta, out):
             nc.sync.dma_start(out=bet[:], in_=beta.rearrange("(t p) -> p t", p=P))
         load_x(3)
 
+        def by_square(c, t):
+            return c in SQUARED[t]
+
+        n_sq = [len([c for c in range(NCH) if by_square(c, t)]) for t in range(FT)]
+        n_rec = [2 * (NCH - n_sq[t]) + n_sq[t] for t in range(FT)]
+        stats = [const.tile([P, 3 * n_rec[t]], F32, name="stats%d" % t) for t in range(FT)]
+        sums = [const.tile([P, NCH], F32, name="sums%d" % t) for t in range(FT)]
+        junk = const.tile([P, CH], BF16, name="junk")
+        rec_of = {}
+        for t in range(FT):
+            nc.gpsimd.memset(stats[t][:], float(CH))
+            lo = 0
+            for c in range(NCH):
+                if by_square(c, t):
+                    rec_of[(c, t)] = lo
+                    lo += 3
+            for c in range(NCH):
+                if not by_square(c, t):
+                    rec_of[(c, t)] = lo
+                    lo += 6
+
         ident = const.tile([P, P], F32, name="ident")
         masks.make_identity(nc, ident[:])
         mhalf = const.tile([P, 1], F32, name="mhalf")
@@ -100,7 +123,7 @@ def tile_attention_prop_pa_t_kernel(tc, x, w1, b1, w2, b2, gamma, beta, out):
         bef = const.tile([P, FT], F32, name="bef")
         nc.gpsimd.tensor_copy(out=b1f[:], in_=b1t[:])
         nc.gpsimd.tensor_copy(out=b2f[:], in_=b2t[:])
-        nc.gpsimd.tensor_scalar(out=b2s[:], in0=b2t[:], scalar1=SLOPE - 1.0, scalar2=0.0, op0=ALU.mult, op1=ALU.add)
+        nc.gpsimd.tensor_scalar(out=b2s[:], in0=b2t[:], scalar1=1.0 - SLOPE, scalar2=0.0, op0=ALU.mult, op1=ALU.add)
         for t in range(FT):
             for j in range(2):
                 nc.gpsimd.tensor_scalar(
@@ -153,7 +176,6 @@ def tile_attention_prop_pa_t_kernel(tc, x, w1, b1, w2, b2, gamma, beta, out):
         s2s = {}
         h2s = {}
         obanks = {}
-        stats = [const.tile([P, 6 * NCH], F32, name="stats%d" % t) for t in range(FT)]
         coefs = {}
 
         def t_x(c):
@@ -234,9 +256,9 @@ def tile_attention_prop_pa_t_kernel(tc, x, w1, b1, w2, b2, gamma, beta, out):
             h1qs[c] = (hq, hs)
             nc.vector.quantize_mx(out=hq[:].bitcast(FP8X4), scales=hs[:], in_=h1gs[c][:])
 
-        def m2(c, t):
+        def m2(c, t, pool):
             hq, hs = h1qs[c]
-            bank = pm.tile([P, 512], F32, name="pmb")
+            bank = pool.tile([P, 512], F32, name="ptb" if pool is pt else "pmb")
             m2banks[(c, t)] = bank
             nc.tensor.matmul_mx(
                 out=bank[:],
@@ -256,22 +278,49 @@ def tile_attention_prop_pa_t_kernel(tc, x, w1, b1, w2, b2, gamma, beta, out):
                     out=s[:], in_=m2banks[(c, t)][:], func=ACT.Identity, bias=b2f[:, t : t + 1], scale=1.0
                 )
             else:
-                nc.scalar.activation(
-                    out=s[:], in_=m2banks[(c, t)][:], func=ACT.Identity, bias=b2s[:, t : t + 1], scale=SLOPE
-                )
+                nc.scalar.activation(out=s[:], in_=m2banks[(c, t)][:], func=ACT.Copy, scale=SLOPE)
 
         def st2(c, t, whole):
             h2 = h2p.tile([P, 512], F32, name="h2_%d_%d" % (t, c))
             h2s[(c, t)] = h2
+            sq = by_square(c, t)
+            acc = sums[t][:, c : c + 1] if sq else None
+            s = s2s[(c, t)]
             if whole:
                 nc.vector.scalar_tensor_tensor(
-                    out=h2[:], in0=s2s[(c, t)][:], scalar=SLOPE, in1=s2s[(c, t)][:], op0=ALU.mult, op1=ALU.max
+                    out=h2[:], in0=s[:], scalar=SLOPE, in1=s[:], op0=ALU.mult, op1=ALU.max, accum_out=acc
                 )
             else:
-                nc.vector.tensor_tensor(out=h2[:], in0=m2banks[(c, t)][:], in1=s2s[(c, t)][:], op=ALU.max)
+                nc.vector.scalar_tensor_tensor(
+                    out=h2[:],
+                    in0=m2banks[(c, t)][:],
+                    scalar=b2s[:, t : t + 1],
+                    in1=s[:],
+                    op0=ALU.add,
+                    op1=ALU.max,
+                    accum_out=acc,
+                )
 
         def bn(c, t):
-            nc.vector.bn_stats(out=stats[t][:, 6 * c : 6 * (c + 1)], in_=h2s[(c, t)][:])
+            lo = rec_of[(c, t)]
+            nc.vector.bn_stats(out=stats[t][:, lo : lo + 6], in_=h2s[(c, t)][:])
+
+        def mean_of(c, t):
+            lo = rec_of[(c, t)]
+            nc.scalar.activation(
+                out=stats[t][:, lo + 1 : lo + 2], in_=sums[t][:, c : c + 1], func=ACT.Copy, scale=1.0 / CH
+            )
+
+        def square(c, t):
+            lo = rec_of[(c, t)]
+            nc.scalar.activation(
+                out=junk[:],
+                in_=h2s[(c, t)][:],
+                func=ACT.Square,
+                bias=stats[t][:, lo + 1 : lo + 2],
+                scale=-1.0,
+                accum_out=stats[t][:, lo + 2 : lo + 3],
+            )
 
         def agg(t):
             mv = const.tile([P, 2], F32, name="mv%d" % t)
@@ -296,7 +345,8 @@ def tile_attention_prop_pa_t_kernel(tc, x, w1, b1, w2, b2, gamma, beta, out):
             eng.tensor_scalar(out=h2[:], in0=h2[:], scalar1=ca[:, 0:1], scalar2=cb[:, 0:1], op0=ALU.mult, op1=ALU.add)
 
         def t_o(c, t):
-            bank = pt.tile([P, 512], F32, name="ptb")
+            tail = t == FT - 1 and c % 2 == 1
+            bank = (pm if tail else pt).tile([P, 512], F32, name="pmb" if tail else "ptb")
             obanks[(c, t)] = bank
             h2 = h2s[(c, t)]
             for i in range(RT):
@@ -304,7 +354,7 @@ def tile_attention_prop_pa_t_kernel(tc, x, w1, b1, w2, b2, gamma, beta, out):
 
         def ex(c, t):
             ost = ostp.tile([P, 512], F32, name="ost")
-            if t == FT - 1 and c % 2 == 1:
+            if t == FT - 1 and c >= TAIL_C:
                 nc.vector.tensor_copy(out=ost[:], in_=obanks[(c, t)][:])
             else:
                 nc.scalar.copy(out=ost[:], in_=obanks[(c, t)][:])
@@ -314,10 +364,11 @@ def tile_attention_prop_pa_t_kernel(tc, x, w1, b1, w2, b2, gamma, beta, out):
 
         waiting = [(c, t) for t in range(FT) for c in range(NCH)]
         quantised = []
-        statq = []
-        done_stats = []
+        bnq = []
+        sqq = []
+        left = {t: NCH for t in range(FT)}
+        aggq = []
         outq = []
-        whole_of = {}
         pos = {"g": 0}
 
         def take(n):
@@ -328,22 +379,42 @@ def tile_attention_prop_pa_t_kernel(tc, x, w1, b1, w2, b2, gamma, beta, out):
                     waiting.remove(u)
             return got
 
+        def counted(t):
+            left[t] -= 1
+            if left[t] == 0:
+                aggq.append(t)
+
         def flush_bn(keep):
-            while len(statq) > keep:
-                c, t = statq.pop(0)
+            while len(bnq) > keep:
+                c, t = bnq.pop(0)
                 bn(c, t)
-                done_stats.append((c, t))
-                if len([u for u in done_stats if u[1] == t]) == NCH:
-                    agg(t)
-                    for cc in range(NCH):
-                        norm(cc, t, nc.gpsimd if t < FT - 1 else nc.vector)
-                        outq.append(((cc, t), pos["g"]))
+                counted(t)
+
+        def flush_sq(keep):
+            todo = sqq[: len(sqq) - keep]
+            for c, t in todo:
+                mean_of(c, t)
+            for c, t in todo:
+                sqq.remove((c, t))
+                square(c, t)
+                counted(t)
+
+        def flush_agg():
+            while aggq:
+                t = aggq.pop(0)
+                agg(t)
+                for cc in range(NCH):
+                    norm(cc, t, nc.gpsimd if t < FT - 1 else nc.vector)
+                    outq.append(((cc, t), pos["g"]))
 
         def do_st2(u):
-            st2(u[0], u[1], whole_of[u])
-            statq.append(u)
+            st2(u[0], u[1], u[1] == 0)
+            if by_square(u[0], u[1]):
+                sqq.append(u)
+            else:
+                bnq.append(u)
 
-        RIDE = {2: 1, 3: 1, 4: 1, 5: 1, 6: 1, 7: 1}
+        RIDE = {2: 1, 3: 1, 4: 1, 5: 1, 6: 2, 7: 2}
         t_x(0)
         copy_w1(0)
         quant_w1(0)
@@ -372,27 +443,27 @@ def tile_attention_prop_pa_t_kernel(tc, x, w1, b1, w2, b2, gamma, beta, out):
             st1(n)
             xe(n + 2, [0])
             for u in units:
-                m2(u[0], u[1])
-                whole_of[u] = True
-                s2(u[0], u[1], True)
+                m2(u[0], u[1], pt if n + 2 >= NCH else pm)
+                s2(u[0], u[1], u[1] == 0)
             if n + 1 < NCH:
                 m1(n + 1)
             xe(n + 2, [1, 2, 3])
+            flush_sq(0)
             prev = units
             if n >= 1:
                 quantised.append(n - 1)
-        for u in prev:
-            do_st2(u)
+        do_st2(prev[0])
         qh(NCH - 1)
-        quantised.append(NCH - 1)
-        prev = []
-        LAG = 2
-        while waiting or prev or statq or outq:
+        flush_bn(0)
+        prev = prev[1:]
+        LAG = 1
+        while waiting or prev or bnq or sqq or outq:
             pos["g"] += 1
             units = take(GB)
+            if NCH - 1 not in quantised:
+                quantised.append(NCH - 1)
             for u in units:
-                m2(u[0], u[1])
-                whole_of[u] = u[1] == 0
+                m2(u[0], u[1], pm)
             outs = []
             while outq and len(outs) < GB and (pos["g"] - outq[0][1] >= LAG or not waiting):
                 outs.append(outq.pop(0)[0])
@@ -401,10 +472,14 @@ def tile_attention_prop_pa_t_kernel(tc, x, w1, b1, w2, b2, gamma, beta, out):
                 flush_bn(1)
             if not units:
                 flush_bn(0)
+            flush_agg()
             for u in outs:
                 t_o(u[0], u[1])
             for u in units:
-                s2(u[0], u[1], whole_of[u])
+                s2(u[0], u[1], u[1] == 0)
+            flush_sq(0)
             for u in outs:
                 ex(u[0], u[1])
+            if not units:
+                flush_agg()
             prev = units

@@ -22,7 +22,8 @@ EPS = 1e-5
 SLOPE = 0.01
 FLOPS = 2 * NQ * QS * F + 2 * NQ * F * F
 
-SQUARED = {0: (2, 4), 1: (0, 1, 2), 2: (), 3: ()}
+SQUARED = {0: (), 1: (0, 1, 2), 2: (), 3: ()}
+LATE = 2
 TAIL_C = 5
 GB = 2
 
@@ -67,11 +68,11 @@ def tile_attention_prop_pa_t_kernel(tc, x, w1, b1, w2, b2, gamma, beta, out):
         def load_x(c):
             xc = xin.tile([P, RT * QS], BF16, name="xc")
             xt_tiles[c] = xc
-            if c == 0:
+            if c <= 1:
                 for i in range(RT):
-                    if i % 2 == 0:
+                    if c == 0 and i % 2 == 0:
                         load_w1(i // 2)
-                    nc.sync.dma_start(out=xc[:, QS * i : QS * (i + 1)], in_=x_v[:, i, :])
+                    nc.sync.dma_start(out=xc[:, QS * i : QS * (i + 1)], in_=x_v[:, RT * c + i, :])
             else:
                 nc.sync.dma_start(
                     out=xc[:].rearrange("p (i k) -> p i k", i=RT), in_=x_v[:, RT * c : RT * (c + 1), :]
@@ -330,12 +331,13 @@ def tile_attention_prop_pa_t_kernel(tc, x, w1, b1, w2, b2, gamma, beta, out):
             cb = const.tile([P, 1], F32, name="cb%d" % t)
             coefs[t] = (ca, cb)
             nc.vector.bn_aggr(out=mv[:], in_=stats[t][:])
-            nc.gpsimd.tensor_scalar(out=ve[:], in0=mv[:, 1:2], scalar1=1.0, scalar2=EPS, op0=ALU.mult, op1=ALU.add)
+            eng = nc.gpsimd if t < FT - 1 else nc.vector
+            eng.tensor_scalar(out=ve[:], in0=mv[:, 1:2], scalar1=1.0, scalar2=EPS, op0=ALU.mult, op1=ALU.add)
             nc.gpsimd.tensor_tensor(out=rstd[:], in0=ve[:], in1=mhalf[:], op=ALU.pow)
-            nc.gpsimd.tensor_scalar(
+            eng.tensor_scalar(
                 out=ca[:], in0=gaf[:, 2 * t : 2 * t + 2], scalar1=rstd[:, 0:1], scalar2=0.0, op0=ALU.mult, op1=ALU.add
             )
-            nc.gpsimd.tensor_scalar(
+            eng.tensor_scalar(
                 out=cb[:], in0=mv[:, 0:1], scalar1=ca[:, 1:2], scalar2=bef[:, t : t + 1], op0=ALU.mult, op1=ALU.add
             )
 
@@ -368,6 +370,7 @@ def tile_attention_prop_pa_t_kernel(tc, x, w1, b1, w2, b2, gamma, beta, out):
         sqq = []
         left = {t: NCH for t in range(FT)}
         aggq = []
+        later = []
         outq = []
         pos = {"g": 0}
 
@@ -390,8 +393,7 @@ def tile_attention_prop_pa_t_kernel(tc, x, w1, b1, w2, b2, gamma, beta, out):
                 bn(c, t)
                 counted(t)
 
-        def flush_sq(keep):
-            todo = sqq[: len(sqq) - keep]
+        def flush_sq(todo):
             for c, t in todo:
                 mean_of(c, t)
             for c, t in todo:
@@ -403,7 +405,14 @@ def tile_attention_prop_pa_t_kernel(tc, x, w1, b1, w2, b2, gamma, beta, out):
             while aggq:
                 t = aggq.pop(0)
                 agg(t)
+                for cc, tt in later:
+                    norm(cc, tt, nc.vector)
+                    outq.append(((cc, tt), pos["g"]))
+                later.clear()
                 for cc in range(NCH):
+                    if t == FT - 2 and cc >= NCH - LATE:
+                        later.append((cc, t))
+                        continue
                     norm(cc, t, nc.gpsimd if t < FT - 1 else nc.vector)
                     outq.append(((cc, t), pos["g"]))
 
@@ -448,7 +457,7 @@ def tile_attention_prop_pa_t_kernel(tc, x, w1, b1, w2, b2, gamma, beta, out):
             if n + 1 < NCH:
                 m1(n + 1)
             xe(n + 2, [1, 2, 3])
-            flush_sq(0)
+            flush_sq(list(sqq))
             prev = units
             if n >= 1:
                 quantised.append(n - 1)
@@ -456,10 +465,11 @@ def tile_attention_prop_pa_t_kernel(tc, x, w1, b1, w2, b2, gamma, beta, out):
         qh(NCH - 1)
         flush_bn(0)
         prev = prev[1:]
-        LAG = 1
+        LAG = 2
         while waiting or prev or bnq or sqq or outq:
             pos["g"] += 1
             units = take(GB)
+            squares = list(sqq)
             if NCH - 1 not in quantised:
                 quantised.append(NCH - 1)
             for u in units:
@@ -477,7 +487,7 @@ def tile_attention_prop_pa_t_kernel(tc, x, w1, b1, w2, b2, gamma, beta, out):
                 t_o(u[0], u[1])
             for u in units:
                 s2(u[0], u[1], u[1] == 0)
-            flush_sq(0)
+            flush_sq(squares)
             for u in outs:
                 ex(u[0], u[1])
             if not units:

@@ -25,6 +25,11 @@ FLOPS = 2 * NQ * QS * F + 2 * NQ * F * F
 SQUARED = {0: (), 1: (0, 1, 2), 2: (), 3: ()}
 LATE = 2
 TAIL_C = 5
+ND = 4
+NA = 1
+NA2 = 2
+NG = 1
+NT = 0
 GB = 2
 
 
@@ -99,6 +104,8 @@ def tile_attention_prop_pa_t_kernel(tc, x, w1, b1, w2, b2, gamma, beta, out):
         n_rec = [2 * (NCH - n_sq[t]) + n_sq[t] for t in range(FT)]
         stats = [const.tile([P, 3 * n_rec[t]], F32, name="stats%d" % t) for t in range(FT)]
         sums = [const.tile([P, NCH], F32, name="sums%d" % t) for t in range(FT)]
+        warm = const.tile([P, CH], BF16, name="warm")
+        nc.gpsimd.memset(warm[:], 1.0)
         junk = const.tile([P, CH], BF16, name="junk")
         rec_of = {}
         for t in range(FT):
@@ -179,20 +186,26 @@ def tile_attention_prop_pa_t_kernel(tc, x, w1, b1, w2, b2, gamma, beta, out):
         obanks = {}
         coefs = {}
 
-        def t_x(c):
+        def keep_busy(bank, n):
+            for j in range(n):
+                nc.tensor.matmul(bank[:], lhsT=warm[:, 0:P], rhs=warm[:], start=True, stop=True)
+
+        def t_x(c, tiles, busy):
             if c >= NCH:
                 return
             xw = xt_tiles[c][:].bitcast(F32)
-            for i in range(RT):
+            for i in tiles:
                 bank = pt.tile([P, 512], F32, name="ptb")
                 xbanks[(c, i)] = bank
+                if i == tiles[0]:
+                    keep_busy(bank, busy)
                 for q in range(4):
                     nc.tensor.transpose(
                         bank[:, P * q : P * (q + 1)],
                         xw[:, 512 * i + 256 * (q // 2) + q % 2 : 512 * i + 256 * (q // 2 + 1) : 2],
                         ident[:],
                     )
-            if c + 4 < NCH:
+            if c + 4 < NCH and RT - 1 in tiles:
                 load_x(c + 4)
 
         def xe(c, tiles):
@@ -346,10 +359,11 @@ def tile_attention_prop_pa_t_kernel(tc, x, w1, b1, w2, b2, gamma, beta, out):
             h2 = h2s[(c, t)]
             eng.tensor_scalar(out=h2[:], in0=h2[:], scalar1=ca[:, 0:1], scalar2=cb[:, 0:1], op0=ALU.mult, op1=ALU.add)
 
-        def t_o(c, t):
+        def t_o(c, t, busy):
             tail = t == FT - 1 and c % 2 == 1
             bank = (pm if tail else pt).tile([P, 512], F32, name="pmb" if tail else "ptb")
             obanks[(c, t)] = bank
+            keep_busy(bank, busy)
             h2 = h2s[(c, t)]
             for i in range(RT):
                 nc.tensor.transpose(bank[:, P * i : P * (i + 1)], h2[:, P * i : P * (i + 1)], ident[:])
@@ -424,21 +438,24 @@ def tile_attention_prop_pa_t_kernel(tc, x, w1, b1, w2, b2, gamma, beta, out):
                 bnq.append(u)
 
         RIDE = {2: 1, 3: 1, 4: 1, 5: 1, 6: 2, 7: 2}
-        t_x(0)
+        t_x(0, range(RT), ND)
         copy_w1(0)
         quant_w1(0)
         copy_w1(1)
         xe(0, range(RT))
         quant_w1(1)
-        t_x(1)
+        t_x(1, range(RT), 0)
         qx(0)
         m1(0)
         xe(1, range(RT))
         copy_w2()
         prev = []
         for n in range(NCH):
-            t_x(n + 2)
             units = take(RIDE.get(n, 0))
+            t_x(n + 2, [0, 1], 0)
+            for u in units:
+                m2(u[0], u[1], pt if n + 2 >= NCH else pm)
+            t_x(n + 2, [2, 3], NA if units else NA2)
             for u in prev:
                 do_st2(u)
             if n + 1 < NCH:
@@ -452,7 +469,6 @@ def tile_attention_prop_pa_t_kernel(tc, x, w1, b1, w2, b2, gamma, beta, out):
             st1(n)
             xe(n + 2, [0])
             for u in units:
-                m2(u[0], u[1], pt if n + 2 >= NCH else pm)
                 s2(u[0], u[1], u[1] == 0)
             if n + 1 < NCH:
                 m1(n + 1)
@@ -484,7 +500,7 @@ def tile_attention_prop_pa_t_kernel(tc, x, w1, b1, w2, b2, gamma, beta, out):
                 flush_bn(0)
             flush_agg()
             for u in outs:
-                t_o(u[0], u[1])
+                t_o(u[0], u[1], NG if units else NT)
             for u in units:
                 s2(u[0], u[1], u[1] == 0)
             flush_sq(squares)

@@ -70,32 +70,42 @@ def tile_attention_prop_pa_t_kernel(tc, x, w1, b1, w2, b2, gamma, beta, out):
 
         xt_tiles = {}
 
+        w2raw = wts.tile([P, 2048], BF16, name="w2raw")
+
+        def load_tile(c, i):
+            nc.sync.dma_start(out=xt_tiles[c][:, QS * i : QS * (i + 1)], in_=x_v[:, RT * c + i, :])
+
         def load_x(c):
-            xc = xin.tile([P, RT * QS], BF16, name="xc")
-            xt_tiles[c] = xc
-            if c <= 1:
-                for i in range(RT):
-                    if c == 0 and i % 2 == 0:
-                        load_w1(i // 2)
-                    nc.sync.dma_start(out=xc[:, QS * i : QS * (i + 1)], in_=x_v[:, RT * c + i, :])
-            else:
+            if c not in xt_tiles:
+                xt_tiles[c] = xin.tile([P, RT * QS], BF16, name="xc")
+            if c > 1:
                 nc.sync.dma_start(
-                    out=xc[:].rearrange("p (i k) -> p i k", i=RT), in_=x_v[:, RT * c : RT * (c + 1), :]
+                    out=xt_tiles[c][:].rearrange("p (i k) -> p i k", i=RT), in_=x_v[:, RT * c : RT * (c + 1), :]
                 )
+
+        def load_column(tile, vec):
+            with nc.allow_non_contiguous_dma(reason="512 values, one to a partition and feature tile"):
+                nc.sync.dma_start(out=tile[:], in_=vec.rearrange("(t p) -> p t", p=P))
 
         load_x(0)
         load_x(1)
-        w2raw = wts.tile([P, 2048], BF16, name="w2raw")
+        load_w1(0)
+        load_tile(0, 0)
+        load_tile(0, 1)
+        nc.sync.dma_start(out=b1t[:], in_=b1.rearrange("(p t) -> p t", t=FT))
+        load_w1(1)
+        load_tile(0, 2)
+        load_tile(0, 3)
+        load_tile(1, 0)
+        load_tile(1, 1)
+        load_tile(1, 2)
+        load_tile(1, 3)
         nc.sync.dma_start(
             out=w2raw[:].rearrange("p (t c) -> p t c", t=4), in_=w2.rearrange("(p t) c -> p t c", t=4)
         )
-        nc.sync.dma_start(out=b1t[:], in_=b1.rearrange("(p t) -> p t", t=FT))
         load_x(2)
-        with nc.allow_non_contiguous_dma(reason="512 values, one to a partition and feature tile"):
-            nc.sync.dma_start(out=b2t[:], in_=b2.rearrange("(t p) -> p t", p=P))
-            nc.sync.dma_start(out=gat[:], in_=gamma.rearrange("(t p) -> p t", p=P))
-            nc.sync.dma_start(out=bet[:], in_=beta.rearrange("(t p) -> p t", p=P))
         load_x(3)
+        load_column(b2t, b2)
 
         def by_square(c, t):
             return c in SQUARED[t]
@@ -124,25 +134,23 @@ def tile_attention_prop_pa_t_kernel(tc, x, w1, b1, w2, b2, gamma, beta, out):
         masks.make_identity(nc, ident[:])
         mhalf = const.tile([P, 1], F32, name="mhalf")
         nc.gpsimd.memset(mhalf[:], -0.5)
-        b1f = const.tile([P, FT], F32, name="b1f")
-        b2f = const.tile([P, FT], F32, name="b2f")
         b2s = const.tile([P, FT], F32, name="b2s")
         gaf = const.tile([P, 2 * FT], F32, name="gaf")
         bef = const.tile([P, FT], F32, name="bef")
-        nc.gpsimd.tensor_copy(out=b1f[:], in_=b1t[:])
-        nc.gpsimd.tensor_copy(out=b2f[:], in_=b2t[:])
         nc.gpsimd.tensor_scalar(out=b2s[:], in0=b2t[:], scalar1=1.0 - SLOPE, scalar2=0.0, op0=ALU.mult, op1=ALU.add)
-        for t in range(FT):
-            for j in range(2):
-                nc.gpsimd.tensor_scalar(
-                    out=gaf[:, 2 * t + j : 2 * t + j + 1],
-                    in0=gat[:, t : t + 1],
-                    scalar1=1.0 - 2.0 * j,
-                    scalar2=0.0,
-                    op0=ALU.mult,
-                    op1=ALU.add,
-                )
-        nc.gpsimd.tensor_copy(out=bef[:], in_=bet[:])
+        def prep_gamma():
+            for t in range(FT):
+                for j in range(2):
+                    nc.gpsimd.tensor_scalar(
+                        out=gaf[:, 2 * t + j : 2 * t + j + 1],
+                        in0=gat[:, t : t + 1],
+                        scalar1=1.0 - 2.0 * j,
+                        scalar2=0.0,
+                        op0=ALU.mult,
+                        op1=ALU.add,
+                    )
+            nc.gpsimd.tensor_copy(out=bef[:], in_=bet[:])
+
 
         w1g = wts.tile([P, 4096], BF16, name="w1g", align_bytes=64)
         w1q = wts.tile([P, 1024], U32, name="w1q", align_bytes=64)
@@ -207,6 +215,10 @@ def tile_attention_prop_pa_t_kernel(tc, x, w1, b1, w2, b2, gamma, beta, out):
                     )
             if c + 4 < NCH and RT - 1 in tiles:
                 load_x(c + 4)
+                if c + 4 == NCH - 1:
+                    load_column(gat, gamma)
+                    load_column(bet, beta)
+                    prep_gamma()
 
         def xe(c, tiles):
             if c >= NCH:
@@ -252,7 +264,7 @@ def tile_attention_prop_pa_t_kernel(tc, x, w1, b1, w2, b2, gamma, beta, out):
                     out=v1[:, 512 * t : 512 * (t + 1)],
                     in_=m1banks[(c, t)][:],
                     func=ACT.Identity,
-                    bias=b1f[:, t : t + 1],
+                    bias=b1t[:, t : t + 1],
                     scale=1.0,
                 )
 
@@ -289,7 +301,7 @@ def tile_attention_prop_pa_t_kernel(tc, x, w1, b1, w2, b2, gamma, beta, out):
             s2s[(c, t)] = s
             if whole:
                 nc.scalar.activation(
-                    out=s[:], in_=m2banks[(c, t)][:], func=ACT.Identity, bias=b2f[:, t : t + 1], scale=1.0
+                    out=s[:], in_=m2banks[(c, t)][:], func=ACT.Identity, bias=b2t[:, t : t + 1], scale=1.0
                 )
             else:
                 nc.scalar.activation(out=s[:], in_=m2banks[(c, t)][:], func=ACT.Copy, scale=SLOPE)

@@ -22,7 +22,7 @@ EPS = 1e-5
 SLOPE = 0.01
 FLOPS = 2 * NQ * QS * F + 2 * NQ * F * F
 
-SQUARED = {0: (), 1: (0, 1, 2), 2: (), 3: ()}
+SQUARED = {0: (2, 4), 1: (0, 1, 2), 2: (), 3: ()}
 LATE = 2
 TAIL_C = 5
 ND = 4
@@ -72,16 +72,17 @@ def tile_attention_prop_pa_t_kernel(tc, x, w1, b1, w2, b2, gamma, beta, out):
 
         w2raw = wts.tile([P, 2048], BF16, name="w2raw")
 
-        def load_tile(c, i):
-            nc.sync.dma_start(out=xt_tiles[c][:, QS * i : QS * (i + 1)], in_=x_v[:, RT * c + i, :])
+        def load_tiles(c, lo, hi):
+            nc.sync.dma_start(
+                out=xt_tiles[c][:, QS * lo : QS * hi].rearrange("p (i k) -> p i k", i=hi - lo),
+                in_=x_v[:, RT * c + lo : RT * c + hi, :],
+            )
 
         def load_x(c):
             if c not in xt_tiles:
                 xt_tiles[c] = xin.tile([P, RT * QS], BF16, name="xc")
             if c > 1:
-                nc.sync.dma_start(
-                    out=xt_tiles[c][:].rearrange("p (i k) -> p i k", i=RT), in_=x_v[:, RT * c : RT * (c + 1), :]
-                )
+                load_tiles(c, 0, RT)
 
         def load_column(tile, vec):
             with nc.allow_non_contiguous_dma(reason="512 values, one to a partition and feature tile"):
@@ -90,16 +91,13 @@ def tile_attention_prop_pa_t_kernel(tc, x, w1, b1, w2, b2, gamma, beta, out):
         load_x(0)
         load_x(1)
         load_w1(0)
-        load_tile(0, 0)
-        load_tile(0, 1)
-        nc.sync.dma_start(out=b1t[:], in_=b1.rearrange("(p t) -> p t", t=FT))
+        load_tiles(0, 0, 1)
+        load_tiles(0, 1, 2)
         load_w1(1)
-        load_tile(0, 2)
-        load_tile(0, 3)
-        load_tile(1, 0)
-        load_tile(1, 1)
-        load_tile(1, 2)
-        load_tile(1, 3)
+        load_tiles(0, 2, 4)
+        nc.sync.dma_start(out=b1t[:], in_=b1.rearrange("(p t) -> p t", t=FT))
+        load_tiles(1, 0, 2)
+        load_tiles(1, 2, 4)
         nc.sync.dma_start(
             out=w2raw[:].rearrange("p (t c) -> p t c", t=4), in_=w2.rearrange("(p t) c -> p t c", t=4)
         )

from contextlib import ExitStack

import concourse.masks as masks
import concourse.mybir as mybir

F32 = mybir.dt.float32
BF16 = mybir.dt.bfloat16
U32 = mybir.dt.uint32
U8 = mybir.dt.uint8
FP8X4 = mybir.dt.float8_e4m3fn_x4
ALU = mybir.AluOpType
ACT = mybir.ActivationFunctionType

P = 128
NQ, QS, F = 4096, 1024, 512
CH = 512
NCH = NQ // CH
RT = CH // P
NI = NQ // P
FT = F // P
EPS = 1e-5
SLOPE = 0.01
FLOPS = 2 * NQ * QS * F + 2 * NQ * F * F

SQUARED = {0: (2, 4), 1: (0, 1, 2), 2: (), 3: ()}
LATE = 2
TAIL_C = 5
ND = 4
NA = 1
NA2 = 2
NG = 1
NT = 0
GB = 2


def tile_attention_prop_pa_t_kernel(tc, x, w1, b1, w2, b2, gamma, beta, out):
    nc = tc.nc
    with ExitStack() as ctx:
        const = ctx.enter_context(tc.tile_pool(name="const", bufs=1))
        wts = ctx.enter_context(tc.tile_pool(name="wts", bufs=1))
        xin = ctx.enter_context(tc.tile_pool(name="xin", bufs=4))
        xgp = ctx.enter_context(tc.tile_pool(name="xgp", bufs=2))
        xqp = ctx.enter_context(tc.tile_pool(name="xqp", bufs=3))
        v1p = ctx.enter_context(tc.tile_pool(name="v1p", bufs=2))
        h1gp = ctx.enter_context(tc.tile_pool(name="h1gp", bufs=2))
        h1qp = ctx.enter_context(tc.tile_pool(name="h1qp", bufs=1))
        h2p = ctx.enter_context(tc.tile_pool(name="h2p", bufs=1))
        s2p = ctx.enter_context(tc.tile_pool(name="s2p", bufs=6))
        ostp = ctx.enter_context(tc.tile_pool(name="ostp", bufs=8))
        pt = ctx.enter_context(tc.psum_pool(name="pt", bufs=4))
        pm = ctx.enter_context(tc.psum_pool(name="pm", bufs=4))
        ctx.enter_context(tc.manual_schedule())

        x_v = x.rearrange("(p i) k -> p i k", i=NI)
        out_v = out.rearrange("(p i) f -> p i f", i=NI)

        b1t = const.tile([P, FT], BF16, name="b1t")
        b2t = const.tile([P, FT], BF16, name="b2t")
        gat = const.tile([P, FT], BF16, name="gat")
        bet = const.tile([P, FT], BF16, name="bet")

        w1raw = wts.tile([P, 4096], BF16, name="w1raw")
        w1_v = w1.rearrange("(g q j) c -> q g j c", g=2, q=P, j=4)

        def load_w1(g):
            nc.sync.dma_start(
                out=w1raw[:, 2048 * g : 2048 * (g + 1)].rearrange("p (j c) -> p j c", j=4),
                in_=w1_v[:, g],
            )

        xt_tiles = {}

        w2raw = wts.tile([P, 2048], BF16, name="w2raw")

        def load_tiles(c, lo, hi):
            nc.sync.dma_start(
                out=xt_tiles[c][:, QS * lo : QS * hi].rearrange("p (i k) -> p i k", i=hi - lo),
                in_=x_v[:, RT * c + lo : RT * c + hi, :],
            )

        def load_x(c):
            if c not in xt_tiles:
                xt_tiles[c] = xin.tile([P, RT * QS], BF16, name="xc")
            if c > 1:
                load_tiles(c, 0, RT)

        def load_column(tile, vec):
            with nc.allow_non_contiguous_dma(reason="512 values, one to a partition and feature tile"):
                nc.sync.dma_start(out=tile[:], in_=vec.rearrange("(t p) -> p t", p=P))

        load_x(0)
        load_x(1)
        load_w1(0)
        load_tiles(0, 0, 1)
        load_tiles(0, 1, 2)
        load_w1(1)
        load_tiles(0, 2, 4)
        nc.sync.dma_start(out=b1t[:], in_=b1.rearrange("(p t) -> p t", t=FT))
        load_tiles(1, 0, 2)
        load_tiles(1, 2, 4)
        nc.sync.dma_start(
            out=w2raw[:].rearrange("p (t c) -> p t c", t=4), in_=w2.rearrange("(p t) c -> p t c", t=4)
        )
        load_x(2)
        load_x(3)
        load_column(b2t, b2)

        def by_square(c, t):
            return c in SQUARED[t]

        n_sq = [len([c for c in range(NCH) if by_square(c, t)]) for t in range(FT)]
        n_rec = [2 * (NCH - n_sq[t]) + n_sq[t] for t in range(FT)]
        stats = [const.tile([P, 3 * n_rec[t]], F32, name="stats%d" % t) for t in range(FT)]
        sums = [const.tile([P, NCH], F32, name="sums%d" % t) for t in range(FT)]
        warm = const.tile([P, CH], BF16, name="warm")
        nc.gpsimd.memset(warm[:], 1.0)
        junk = const.tile([P, CH], BF16, name="junk")
        rec_of = {}
        for t in range(FT):
            nc.gpsimd.memset(stats[t][:], float(CH))
            lo = 0
            for c in range(NCH):
                if by_square(c, t):
                    rec_of[(c, t)] = lo
                    lo += 3
            for c in range(NCH):
                if not by_square(c, t):
                    rec_of[(c, t)] = lo
                    lo += 6

        ident = const.tile([P, P], F32, name="ident")
        masks.make_identity(nc, ident[:])
        mhalf = const.tile([P, 1], F32, name="mhalf")
        nc.gpsimd.memset(mhalf[:], -0.5)
        b2s = const.tile([P, FT], F32, name="b2s")
        gaf = const.tile([P, 2 * FT], F32, name="gaf")
        bef = const.tile([P, FT], F32, name="bef")
        nc.gpsimd.tensor_scalar(out=b2s[:], in0=b2t[:], scalar1=1.0 - SLOPE, scalar2=0.0, op0=ALU.mult, op1=ALU.add)
        def prep_gamma():
            for t in range(FT):
                for j in range(2):
                    nc.gpsimd.tensor_scalar(
                        out=gaf[:, 2 * t + j : 2 * t + j + 1],
                        in0=gat[:, t : t + 1],
                        scalar1=1.0 - 2.0 * j,
                        scalar2=0.0,
                        op0=ALU.mult,
                        op1=ALU.add,
                    )
            nc.gpsimd.tensor_copy(out=bef[:], in_=bet[:])


        w1g = wts.tile([P, 4096], BF16, name="w1g", align_bytes=64)
        w1q = wts.tile([P, 1024], U32, name="w1q", align_bytes=64)
        w1s = wts.tile([P, 1024], U8, name="w1s", align_bytes=64)

        def copy_w1(g):
            nc.vector.tensor_copy(
                out=w1g[:, 2048 * g : 2048 * (g + 1)].rearrange("p (t m j) -> p t m j", t=4, m=P, j=4),
                in_=w1raw[:, 2048 * g : 2048 * (g + 1)].rearrange("p (j m t) -> p t m j", j=4, m=P, t=4),
            )

        def quant_w1(g):
            nc.vector.quantize_mx(
                out=w1q[:, 512 * g : 512 * (g + 1)].bitcast(FP8X4),
                scales=w1s[:, 512 * g : 512 * (g + 1)],
                in_=w1g[:, 2048 * g : 2048 * (g + 1)],
            )

        w2g = wts.tile([P, 2048], BF16, name="w2g", align_bytes=64)
        w2q = wts.tile([P, 512], U32, name="w2q", align_bytes=64)
        w2s = wts.tile([P, 512], U8, name="w2s", align_bytes=64)

        def copy_w2():
            nc.vector.tensor_copy(
                out=w2g[:].rearrange("p (c t) -> p c t", t=4), in_=w2raw[:].rearrange("p (t c) -> p c t", t=4)
            )

        def quant_w2():
            nc.vector.quantize_mx(out=w2q[:].bitcast(FP8X4), scales=w2s[:], in_=w2g[:])

        xbanks = {}
        xgs = {}
        xqs = {}
        m1banks = {}
        v1s = {}
        h1gs = {}
        h1qs = {}
        m2banks = {}
        s2s = {}
        h2s = {}
        obanks = {}
        coefs = {}

        def keep_busy(bank, n):
            for j in range(n):
                nc.tensor.matmul(bank[:], lhsT=warm[:, 0:P], rhs=warm[:], start=True, stop=True)

        def t_x(c, tiles, busy):
            if c >= NCH:
                return
            xw = xt_tiles[c][:].bitcast(F32)
            for i in tiles:
                bank = pt.tile([P, 512], F32, name="ptb")
                xbanks[(c, i)] = bank
                if i == tiles[0]:
                    keep_busy(bank, busy)
                for q in range(4):
                    nc.tensor.transpose(
                        bank[:, P * q : P * (q + 1)],
                        xw[:, 512 * i + 256 * (q // 2) + q % 2 : 512 * i + 256 * (q // 2 + 1) : 2],
                        ident[:],
                    )
            if c + 4 < NCH and RT - 1 in tiles:
                load_x(c + 4)
                if c + 4 == NCH - 1:
                    load_column(gat, gamma)
                    load_column(bet, beta)
                    prep_gamma()

        def xe(c, tiles):
            if c >= NCH:
                return
            if 0 in tiles:
                xg = xgp.tile([P, 4096], BF16, name="xg", align_bytes=64)
                xgs[c] = xg
            xg32 = xgs[c][:].bitcast(F32).rearrange("p (g r u) -> p g r u", g=2, r=CH, u=2)
            for i in tiles:
                nc.scalar.copy(
                    out=xg32[:, :, P * i : P * (i + 1), :],
                    in_=xbanks[(c, i)][:].rearrange("p (g u r) -> p g r u", g=2, u=2, r=P),
                )

        def qx(c):
            xq = xqp.tile([P, 1024], U32, name="xq", align_bytes=64)
            xs = xqp.tile([P, 1024], U8, name="xs", align_bytes=64)
            xqs[c] = (xq, xs)
            nc.vector.quantize_mx(out=xq[:].bitcast(FP8X4), scales=xs[:], in_=xgs[c][:])

        def m1(c):
            xq, xs = xqs[c]
            for t in range(FT):
                bank = pm.tile([P, 512], F32, name="pmb")
                m1banks[(c, t)] = bank
                for g in range(2):
                    lo = 512 * g + P * t
                    nc.tensor.matmul_mx(
                        out=bank[:],
                        lhsT=w1q[:, lo : lo + P].bitcast(FP8X4),
                        lhsT_scale=w1s[:, lo : lo + P],
                        rhs=xq[:, 512 * g : 512 * (g + 1)].bitcast(FP8X4),
                        rhs_scale=xs[:, 512 * g : 512 * (g + 1)],
                        start=(g == 0),
                        stop=(g == 1),
                    )

        def bias1(c):
            v1 = v1p.tile([P, 2048], F32, name="v1")
            v1s[c] = v1
            for t in range(FT):
                nc.scalar.activation(
                    out=v1[:, 512 * t : 512 * (t + 1)],
                    in_=m1banks[(c, t)][:],
                    func=ACT.Identity,
                    bias=b1t[:, t : t + 1],
                    scale=1.0,
                )

        def st1(c):
            h1g = h1gp.tile([P, 2048], BF16, name="h1g", align_bytes=64)
            h1gs[c] = h1g
            v = v1s[c][:].rearrange("p (t w) -> p w t", t=FT)
            nc.vector.scalar_tensor_tensor(
                out=h1g[:].rearrange("p (w t) -> p w t", t=FT), in0=v, scalar=SLOPE, in1=v, op0=ALU.mult, op1=ALU.max
            )

        def qh(c):
            hq = h1qp.tile([P, 512], U32, name="h1q%d" % c, align_bytes=64)
            hs = h1qp.tile([P, 512], U8, name="h1s%d" % c, align_bytes=64)
            h1qs[c] = (hq, hs)
            nc.vector.quantize_mx(out=hq[:].bitcast(FP8X4), scales=hs[:], in_=h1gs[c][:])

        def m2(c, t, pool):
            hq, hs = h1qs[c]
            bank = pool.tile([P, 512], F32, name="ptb" if pool is pt else "pmb")
            m2banks[(c, t)] = bank
            nc.tensor.matmul_mx(
                out=bank[:],
                lhsT=w2q[:, P * t : P * (t + 1)].bitcast(FP8X4),
                lhsT_scale=w2s[:, P * t : P * (t + 1)],
                rhs=hq[:].bitcast(FP8X4),
                rhs_scale=hs[:],
                start=True,
                stop=True,
            )

        def s2(c, t, whole):
            s = s2p.tile([P, 512], F32, name="s2")
            s2s[(c, t)] = s
            if whole:
                nc.scalar.activation(
                    out=s[:], in_=m2banks[(c, t)][:], func=ACT.Identity, bias=b2t[:, t : t + 1], scale=1.0
                )
            else:
                nc.scalar.activation(out=s[:], in_=m2banks[(c, t)][:], func=ACT.Copy, scale=SLOPE)

        def st2(c, t, whole):
            h2 = h2p.tile([P, 512], F32, name="h2_%d_%d" % (t, c))
            h2s[(c, t)] = h2
            sq = by_square(c, t)
            acc = sums[t][:, c : c + 1] if sq else None
            s = s2s[(c, t)]
            if whole:
                nc.vector.scalar_tensor_tensor(
                    out=h2[:], in0=s[:], scalar=SLOPE, in1=s[:], op0=ALU.mult, op1=ALU.max, accum_out=acc
                )
            else:
                nc.vector.scalar_tensor_tensor(
                    out=h2[:],
                    in0=m2banks[(c, t)][:],
                    scalar=b2s[:, t : t + 1],
                    in1=s[:],
                    op0=ALU.add,
                    op1=ALU.max,
                    accum_out=acc,
                )

        def bn(c, t):
            lo = rec_of[(c, t)]
            nc.vector.bn_stats(out=stats[t][:, lo : lo + 6], in_=h2s[(c, t)][:])

        def mean_of(c, t):
            lo = rec_of[(c, t)]
            nc.scalar.activation(
                out=stats[t][:, lo + 1 : lo + 2], in_=sums[t][:, c : c + 1], func=ACT.Copy, scale=1.0 / CH
            )

        def square(c, t):
            lo = rec_of[(c, t)]
            nc.scalar.activation(
                out=junk[:],
                in_=h2s[(c, t)][:],
                func=ACT.Square,
                bias=stats[t][:, lo + 1 : lo + 2],
                scale=-1.0,
                accum_out=stats[t][:, lo + 2 : lo + 3],
            )

        def agg(t):
            mv = const.tile([P, 2], F32, name="mv%d" % t)
            ve = const.tile([P, 1], F32, name="ve%d" % t)
            rstd = const.tile([P, 1], F32, name="rstd%d" % t)
            ca = const.tile([P, 2], F32, name="ca%d" % t)
            cb = const.tile([P, 1], F32, name="cb%d" % t)
            coefs[t] = (ca, cb)
            nc.vector.bn_aggr(out=mv[:], in_=stats[t][:])
            eng = nc.gpsimd if t < FT - 1 else nc.vector
            eng.tensor_scalar(out=ve[:], in0=mv[:, 1:2], scalar1=1.0, scalar2=EPS, op0=ALU.mult, op1=ALU.add)
            nc.gpsimd.tensor_tensor(out=rstd[:], in0=ve[:], in1=mhalf[:], op=ALU.pow)
            eng.tensor_scalar(
                out=ca[:], in0=gaf[:, 2 * t : 2 * t + 2], scalar1=rstd[:, 0:1], scalar2=0.0, op0=ALU.mult, op1=ALU.add
            )
            eng.tensor_scalar(
                out=cb[:], in0=mv[:, 0:1], scalar1=ca[:, 1:2], scalar2=bef[:, t : t + 1], op0=ALU.mult, op1=ALU.add
            )

        def norm(c, t, eng):
            ca, cb = coefs[t]
            h2 = h2s[(c, t)]
            eng.tensor_scalar(out=h2[:], in0=h2[:], scalar1=ca[:, 0:1], scalar2=cb[:, 0:1], op0=ALU.mult, op1=ALU.add)

        def t_o(c, t, busy):
            tail = t == FT - 1 and c % 2 == 1
            bank = (pm if tail else pt).tile([P, 512], F32, name="pmb" if tail else "ptb")
            obanks[(c, t)] = bank
            keep_busy(bank, busy)
            h2 = h2s[(c, t)]
            for i in range(RT):
                nc.tensor.transpose(bank[:, P * i : P * (i + 1)], h2[:, P * i : P * (i + 1)], ident[:])

        def ex(c, t):
            ost = ostp.tile([P, 512], F32, name="ost")
            if t == FT - 1 and c >= TAIL_C:
                nc.vector.tensor_copy(out=ost[:], in_=obanks[(c, t)][:])
            else:
                nc.scalar.copy(out=ost[:], in_=obanks[(c, t)][:])
            nc.sync.dma_start(
                out=out_v[:, RT * c : RT * (c + 1), P * t : P * (t + 1)], in_=ost[:].rearrange("p (i f) -> p i f", i=RT)
            )

        waiting = [(c, t) for t in range(FT) for c in range(NCH)]
        quantised = []
        bnq = []
        sqq = []
        left = {t: NCH for t in range(FT)}
        aggq = []
        later = []
        outq = []
        pos = {"g": 0}

        def take(n):
            got = []
            for u in list(waiting):
                if len(got) < n and u[0] in quantised:
                    got.append(u)
                    waiting.remove(u)
            return got

        def counted(t):
            left[t] -= 1
            if left[t] == 0:
                aggq.append(t)

        def flush_bn(keep):
            while len(bnq) > keep:
                c, t = bnq.pop(0)
                bn(c, t)
                counted(t)

        def flush_sq(todo):
            for c, t in todo:
                mean_of(c, t)
            for c, t in todo:
                sqq.remove((c, t))
                square(c, t)
                counted(t)

        def flush_agg():
            while aggq:
                t = aggq.pop(0)
                agg(t)
                for cc, tt in later:
                    norm(cc, tt, nc.vector)
                    outq.append(((cc, tt), pos["g"]))
                later.clear()
                for cc in range(NCH):
                    if t == FT - 2 and cc >= NCH - LATE:
                        later.append((cc, t))
                        continue
                    norm(cc, t, nc.gpsimd if t < FT - 1 else nc.vector)
                    outq.append(((cc, t), pos["g"]))

        def do_st2(u):
            st2(u[0], u[1], u[1] == 0)
            if by_square(u[0], u[1]):
                sqq.append(u)
            else:
                bnq.append(u)

        RIDE = {2: 1, 3: 1, 4: 1, 5: 1, 6: 2, 7: 2}
        t_x(0, range(RT), ND)
        copy_w1(0)
        quant_w1(0)
        copy_w1(1)
        xe(0, range(RT))
        quant_w1(1)
        t_x(1, range(RT), 0)
        qx(0)
        m1(0)
        xe(1, range(RT))
        copy_w2()
        prev = []
        for n in range(NCH):
            units = take(RIDE.get(n, 0))
            t_x(n + 2, [0, 1], 0)
            for u in units:
                m2(u[0], u[1], pt if n + 2 >= NCH else pm)
            t_x(n + 2, [2, 3], NA if units else NA2)
            for u in prev:
                do_st2(u)
            if n + 1 < NCH:
                qx(n + 1)
            if n == 0:
                quant_w2()
            if n >= 1:
                qh(n - 1)
            flush_bn(0)
            bias1(n)
            st1(n)
            xe(n + 2, [0])
            for u in units:
                s2(u[0], u[1], u[1] == 0)
            if n + 1 < NCH:
                m1(n + 1)
            xe(n + 2, [1, 2, 3])
            flush_sq(list(sqq))
            prev = units
            if n >= 1:
                quantised.append(n - 1)
        do_st2(prev[0])
        qh(NCH - 1)
        flush_bn(0)
        prev = prev[1:]
        LAG = 2
        while waiting or prev or bnq or sqq or outq:
            pos["g"] += 1
            units = take(GB)
            squares = list(sqq)
            if NCH - 1 not in quantised:
                quantised.append(NCH - 1)
            for u in units:
                m2(u[0], u[1], pm)
            outs = []
            while outq and len(outs) < GB and (pos["g"] - outq[0][1] >= LAG or not waiting):
                outs.append(outq.pop(0)[0])
            for u in prev:
                do_st2(u)
                flush_bn(1)
            if not units:
                flush_bn(0)
            flush_agg()
            for u in outs:
                t_o(u[0], u[1], NG if units else NT)
            for u in units:
                s2(u[0], u[1], u[1] == 0)
            flush_sq(squares)
            for u in outs:
                ex(u[0], u[1])
            if not units:
                flush_agg()
            prev = units
